import numpy as np
import ml_dtypes


def mxq(x, axis, fmt="e4m3"):
    dtype, down = {"e4m3": (ml_dtypes.float8_e4m3fn, 7), "e5m2": (ml_dtypes.float8_e5m2, 14)}[fmt]
    v = np.moveaxis(np.asarray(x, np.float32).astype(ml_dtypes.bfloat16).astype(np.float64), axis, -1)
    blocks = v.reshape(v.shape[:-1] + (-1, 32))
    amax = np.abs(blocks).max(-1, keepdims=True)
    byte = np.maximum(np.where(amax > 0, np.frexp(amax)[1] - 1 + 127, 0) - down, 1)
    scale = np.exp2(byte - 127.0)
    codes = (blocks / scale).astype(np.float32).astype(dtype).astype(np.float64)
    return np.moveaxis((codes * scale).reshape(v.shape), -1, axis)


WIDE = False


def mx_kscale(k):
    if not WIDE:
        return np.ones(k)
    levels = np.array([10, -10, 5, -5, 0])
    a = np.random.permutation(np.resize(levels, k // 512 * 4)).reshape(k // 512, 4)
    idx = np.arange(k)
    return np.exp2(a[idx // 512, idx % 128 // 32])


BF16 = ml_dtypes.bfloat16


def bf(x):
    return np.asarray(x, np.float32).astype(BF16)


def f64(x):
    return np.asarray(x).astype(np.float64)


B, D, F, M, BLK = 128, 31, 512, 256, 32
DP = D + 1
FUSED = DP * DP * DP
OS = 0.75
W1S = (1.0 + D * OS * OS / 2.0) ** -1.5


def wide_factors():
    s = mx_kscale(FUSED)
    if DP % BLK == 0:
        return np.ones(DP), np.append(s[::DP][:D], 1.0)
    return np.append(s[::DP * DP][:D], 1.0), np.ones(DP)


def stream():
    return np.maximum(np.random.standard_normal((B, D)) * OS, 0.0)


def setup_inputs():
    a, b = wide_factors()
    t = mx_kscale(F)
    col = (a[:, None, None] * b[None, :, None] * np.ones(DP)).reshape(FUSED)
    return {
        'o1': bf(stream() * a[:D]),
        'o2': bf(stream() * b[:D]),
        'o3': bf(stream()),
        'We1': bf(np.random.standard_normal((F, FUSED)) * W1S * t[:, None] / col),
        'be1': bf(np.random.standard_normal(F) * 0.2 * t),
        'We2': bf(np.random.standard_normal((M, F)) * np.sqrt(2.0 / F) / t),
        'be2': bf(np.random.standard_normal(M) * 0.2),
    }


def with_ones(o):
    return np.concatenate([o, np.ones((o.shape[0], 1))], axis=1)


def reference(o1, o2, o3, We1, be1, We2, be2):
    p1, p2, p3 = with_ones(f64(o1)), with_ones(f64(o2)), with_ones(f64(o3))
    o123 = (p1[:, :, None, None] * p2[:, None, :, None] * p3[:, None, None, :]).reshape(p1.shape[0], -1)
    h = np.maximum((mxq(o123, 1, 'e4m3') @ mxq(f64(We1), 1, 'e4m3').T) + f64(be1), 0.0)
    return np.maximum((mxq(h, 1, 'e4m3') @ mxq(f64(We2), 1, 'e4m3').T) + f64(be2), 0.0)

@@ -1,0 +1,284 @@
+from contextlib import ExitStack
+
+import concourse.bass as bass
+import concourse.mybir as mybir
+import concourse.tile as tile
+from concourse.masks import make_identity
+
+F32 = mybir.dt.float32
+BF16 = mybir.dt.bfloat16
+U32 = mybir.dt.uint32
+U8 = mybir.dt.uint8
+FP8X4 = mybir.dt.float8_e4m3fn_x4
+ALU = mybir.AluOpType
+ACT = mybir.ActivationFunctionType
+
+P = 128
+B = 128
+DP = 32
+F = 512
+M = 256
+FUSED = DP * DP * DP
+ROUNDS = 32
+FLOPS = 2 * B * FUSED * F + 2 * B * F * M
+
+RANGES = [1, 1, 2, 4, 4, 4, 4, 4, 4, 2, 1, 1]
+W_BUFS = {1: 2, 2: 1, 4: 3}
+LEAD = 6
+
+
+def tile_tensor_fusion_pa_kernel(tc, o1, o2, o3, We1, be1, We2, be2, out):
+    nc = tc.nc
+    with ExitStack() as ctx:
+        ctx.enter_context(tc.manual_schedule())
+        const = ctx.enter_context(tc.tile_pool(name="const", bufs=1))
+        wpools = {}
+        for n in (1, 2, 4):
+            wpools[n] = ctx.enter_context(tc.tile_pool(name="w%d" % n, bufs=W_BUFS[n]))
+        gpool = ctx.enter_context(tc.tile_pool(name="grouped", bufs=3))
+        cpool = ctx.enter_context(tc.tile_pool(name="wcodes", bufs=3))
+        spool = ctx.enter_context(tc.tile_pool(name="fstage", bufs=2))
+        fpool = ctx.enter_context(tc.tile_pool(name="fcodes", bufs=2))
+        hps = ctx.enter_context(tc.psum_pool(name="hps", bufs=1))
+        pbps = ctx.enter_context(tc.psum_pool(name="pbps", bufs=2))
+        tps = ctx.enter_context(tc.psum_pool(name="tps", bufs=5))
+
+        ident_f = const.tile([P, P], F32, name="ident_f")
+        make_identity(nc, ident_f[:])
+        ident_b = const.tile([P, P], BF16, name="ident_b")
+        make_identity(nc, ident_b[:])
+
+        oraw = const.tile([P, 3, DP], BF16, name="oraw")
+        p_all = const.tile([P, 3, DP], BF16, name="p_all")
+        nc.vector.memset(p_all[:], 1.0)
+        nc.sync.dma_start(out=oraw[:, 1, 0:31], in_=o2)
+        nc.sync.dma_start(out=oraw[:, 2, 0:31], in_=o3)
+        nc.sync.dma_start(out=oraw[:, 0, 0:31], in_=o1)
+        w2raw = const.tile([P, 2, F], BF16, name="w2raw")
+        be1B = const.tile([P, F], BF16, name="be1B")
+        be2B = const.tile([P, M], BF16, name="be2B")
+
+        we1v = We1.rearrange("(m p) k -> p m k", p=P)
+        starts = []
+        acc = 0
+        for n in RANGES:
+            starts.append(acc)
+            acc += n
+        assert acc == ROUNDS
+        wtiles = {}
+        state = {"next": 0}
+        range_of_round = []
+        for j, n in enumerate(RANGES):
+            for q in range(n):
+                range_of_round.append(j)
+
+        def prev_same(j):
+            same = [x for x in range(j) if RANGES[x] == RANGES[j]]
+            nb = W_BUFS[RANGES[j]]
+            if len(same) < nb:
+                return None
+            return same[len(same) - nb]
+
+        def emit_loads(done_round):
+            while state["next"] < len(RANGES):
+                j = state["next"]
+                pj = prev_same(j)
+                if pj is not None and starts[pj] + RANGES[pj] - 1 > done_round:
+                    return
+                n = RANGES[j]
+                wt = wpools[n].tile([P, 4, n * 1024], BF16, name="wt%d" % n, tag="wt%d" % n)
+                nc.sync.dma_start(out=wt[:], in_=we1v[:, :, starts[j] * 1024:(starts[j] + n) * 1024])
+                wtiles[j] = wt[:].bitcast(F32)
+                if j == 5:
+                    nc.sync.dma_start(out=w2raw[:], in_=We2.rearrange("(a p) f -> p a f", p=P))
+                    nc.sync.dma_start(out=be1B[:], in_=be1.partition_broadcast(P))
+                    nc.sync.dma_start(out=be2B[:], in_=be2.partition_broadcast(P))
+                state["next"] = j + 1
+
+        emit_loads(-1)
+
+        nc.vector.tensor_copy(out=p_all[:, :, 0:31], in_=oraw[:, :, 0:31])
+        gb = const.tile([P, 1024], F32, name="gb")
+        for jh in range(2):
+            nc.vector.tensor_tensor(
+                out=gb[:, 512 * jh:512 * jh + 512].rearrange("p (j k) -> p j k", j=16),
+                in0=p_all[:, 1, 16 * jh:16 * jh + 16].unsqueeze(2).broadcast_to([P, 16, DP]),
+                in1=p_all[:, 2, :].unsqueeze(1).broadcast_to([P, 16, DP]),
+                op=ALU.mult,
+            )
+
+        pbs = {}
+
+        def emit_pb(c):
+            pb = pbps.tile([P, 4, B], F32, name="pb", tag="pb")
+            pbs[c] = pb
+            for il in range(4):
+                i = 4 * c + il
+                if i == 31:
+                    continue
+                nc.tensor.matmul(
+                    out=pb[:, il, :],
+                    lhsT=p_all[:, 0, i:i + 1].to_broadcast([P, P]),
+                    rhs=ident_b[:],
+                    start=True,
+                    stop=True,
+                )
+
+        emit_pb(0)
+        emit_pb(1)
+
+        gT = const.tile([P, 1024], F32, name="gT")
+        for jh in range(2):
+            xg = tps.tile([P, 4, B], F32, name="xg", tag="xt")
+            for t in range(4):
+                u, e = t // 2, t % 2
+                c0 = 512 * jh + 256 * u + e
+                nc.tensor.transpose(out=xg[:, t, :], in_=gb[:, c0:c0 + 255:2], identity=ident_f[:])
+            dst = gT[:, 512 * jh:512 * jh + 512].rearrange("p (b t) -> p b t", t=4)
+            src = xg[:].rearrange("p t b -> p b t")
+            if jh == 0:
+                nc.scalar.copy(out=dst, in_=src)
+            else:
+                nc.vector.tensor_copy(out=dst, in_=src)
+
+        w2g = const.tile([P, 4 * M], BF16, name="w2g", align_bytes=64)
+
+        def emit_w2t():
+            x2 = tps.tile([P, 2, 4, P], BF16, name="x2", tag="xt")
+            for a in range(2):
+                for t in range(4):
+                    nc.tensor.transpose(out=x2[:, a, t, :], in_=w2raw[:, a, 128 * t:128 * t + 128], identity=ident_b[:])
+            nc.scalar.copy(
+                out=w2g[:].rearrange("p (a f t) -> p a f t", a=2, t=4),
+                in_=x2[:].rearrange("p a t f -> p a f t"),
+            )
+
+        w2c = const.tile([P, M], U32, name="w2c", align_bytes=64)
+        w2s = const.tile([P, M], U8, name="w2s", align_bytes=64)
+
+        fstages = {}
+        fcodes = {}
+
+        def emit_fg(i):
+            q, il = i // 4, i % 4
+            if il == 0:
+                fstages[q] = spool.tile([P, 4096], BF16, name="fst", tag="fst", align_bytes=64)
+            dst = fstages[q][:, 1024 * il:1024 * il + 1024]
+            if i == 31:
+                nc.scalar.copy(out=dst, in_=gT[:])
+                return
+            nc.vector.tensor_tensor(
+                out=dst.rearrange("p (j b t) -> p j b t", j=2, t=4),
+                in0=gT[:].rearrange("p (j b t) -> p j b t", j=2, t=4),
+                in1=pbs[q][:, il, :].unsqueeze(1).unsqueeze(3).broadcast_to([P, 2, B, 4]),
+                op=ALU.mult,
+            )
+
+        def emit_qf(q):
+            fc = fpool.tile([P, 1024], U32, name="fc", tag="fc", align_bytes=64)
+            fs = fpool.tile([P, 1024], U8, name="fs", tag="fs", align_bytes=64)
+            nc.vector.quantize_mx(out=fc[:].bitcast(FP8X4), scales=fs[:], in_=fstages[q][:])
+            fcodes[q] = (fc, fs)
+
+        groupeds = {}
+        wcodes = {}
+
+        def emit_t_e(r):
+            j = range_of_round[r]
+            ww = wtiles[j]
+            base = (r - starts[j]) * 512
+            grouped = gpool.tile([P, 4096], BF16, name="grouped", tag="grouped", align_bytes=64)
+            groupeds[r] = grouped
+            gw = grouped[:].bitcast(F32)
+            for jh in range(2):
+                for h in range(2):
+                    xt = tps.tile([P, 2, 256], F32, name="xt", tag="xt")
+                    for u in range(2):
+                        for mm in range(2):
+                            c0 = base + 256 * jh + 128 * u
+                            nc.tensor.transpose(
+                                out=xt[:, u, 128 * mm:128 * mm + 128],
+                                in_=ww[:, 2 * h + mm, c0:c0 + 128],
+                                identity=ident_f[:],
+                            )
+                    w0 = 1024 * jh + 512 * h
+                    nc.scalar.copy(
+                        out=gw[:, w0:w0 + 512].rearrange("p (f u) -> p f u", u=2),
+                        in_=xt[:].rearrange("p u f -> p f u"),
+                    )
+
+        def emit_qw(r):
+            wc = cpool.tile([P, 1024], U32, name="wc", tag="wc", align_bytes=64)
+            ws = cpool.tile([P, 1024], U8, name="ws", tag="ws", align_bytes=64)
+            nc.vector.quantize_mx(out=wc[:].bitcast(FP8X4), scales=ws[:], in_=groupeds[r][:])
+            wcodes[r] = (wc, ws)
+
+        hacc = hps.tile([P, F], F32, name="hacc")
+
+        def emit_m(r):
+            wc, ws = wcodes[r]
+            fc, fs = fcodes[r // 4]
+            for jh in range(2):
+                g = 2 * r + jh
+                s0 = ((r % 4) * 2 + jh) * 128
+                nc.tensor.matmul_mx(
+                    out=hacc[:],
+                    lhsT=fc[:, s0:s0 + 128].bitcast(FP8X4),
+                    lhsT_scale=fs[:, s0:s0 + 128],
+                    rhs=wc[:, 512 * jh:512 * jh + 512].bitcast(FP8X4),
+                    rhs_scale=ws[:, 512 * jh:512 * jh + 512],
+                    start=(g == 0),
+                    stop=(g == 2 * ROUNDS - 1),
+                )
+
+        for i in range(LEAD):
+            emit_fg(i)
+        emit_qf(0)
+
+        for s in range(-2, ROUNDS):
+            if s == 12:
+                emit_w2t()
+            if s + 2 < ROUNDS:
+                emit_t_e(s + 2)
+                emit_loads(s + 2)
+            if s < 0:
+                continue
+            emit_qw(s)
+            if s == 13:
+                nc.vector.quantize_mx(out=w2c[:].bitcast(FP8X4), scales=w2s[:], in_=w2g[:])
+            if s >= 2 and (s + 2) % 4 == 0 and (s + 2) // 4 < 8:
+                emit_qf((s + 2) // 4)
+            if s + LEAD < ROUNDS:
+                emit_fg(s + LEAD)
+            emit_m(s)
+            if s % 4 == 0 and s // 4 + 2 < 8:
+                emit_pb(s // 4 + 2)
+
+        hs = const.tile([P, F], BF16, name="hs")
+        nc.vector.tensor_tensor(out=hs[:], in0=hacc[:], in1=be1B[:], op=ALU.add)
+        xh = tps.tile([P, 4, B], BF16, name="xh", tag="xt")
+        for t in range(4):
+            nc.tensor.transpose(out=xh[:, t, :], in_=hs[:, 128 * t:128 * t + 128], identity=ident_b[:])
+        hg = const.tile([P, 4 * B], BF16, name="hg", align_bytes=64)
+        nc.vector.tensor_scalar_max(
+            out=hg[:].rearrange("p (b t) -> p b t", t=4),
+            in0=xh[:].rearrange("p t b -> p b t"),
+            scalar1=0.0,
+        )
+        hc = const.tile([P, B], U32, name="hc", align_bytes=64)
+        hsc = const.tile([P, B], U8, name="hsc", align_bytes=64)
+        nc.vector.quantize_mx(out=hc[:].bitcast(FP8X4), scales=hsc[:], in_=hg[:])
+        o2ps = tps.tile([P, M], F32, name="o2ps", tag="xt")
+        nc.tensor.matmul_mx(
+            out=o2ps[:],
+            lhsT=hc[:].bitcast(FP8X4),
+            lhsT_scale=hsc[:],
+            rhs=w2c[:].bitcast(FP8X4),
+            rhs_scale=w2s[:],
+            start=True,
+            stop=True,
+        )
+        ot = const.tile([P, M], F32, name="ot")
+        nc.vector.tensor_tensor(out=ot[:], in0=o2ps[:], in1=be2B[:], op=ALU.add)
+        nc.vector.tensor_scalar_max(out=ot[:], in0=ot[:], scalar1=0.0)
+        nc.sync.dma_start(out=out, in_=ot[:])

@@ -1,8 +1,6 @@
 from contextlib import ExitStack
 
-import concourse.bass as bass
 import concourse.mybir as mybir
-import concourse.tile as tile
 from concourse.masks import make_identity
 
 F32 = mybir.dt.float32
@@ -11,7 +9,6 @@ U32 = mybir.dt.uint32
 U8 = mybir.dt.uint8
 FP8X4 = mybir.dt.float8_e4m3fn_x4
 ALU = mybir.AluOpType
-ACT = mybir.ActivationFunctionType
 
 P = 128
 B = 128
@@ -22,9 +19,12 @@ FUSED = DP * DP * DP
 ROUNDS = 32
 FLOPS = 2 * B * FUSED * F + 2 * B * F * M
 
-RANGES = [1, 1, 2, 4, 4, 4, 4, 4, 4, 2, 1, 1]
-W_BUFS = {1: 2, 2: 1, 4: 3}
-LEAD = 6
+RANGES = [2, 2, 4, 4, 4, 4, 4, 4, 2, 1, 1]
+W_BUFS = 8
+G_BUFS = 9
+STAGE = 2
+BG = 32
+BV = B - BG
 
 
 def tile_tensor_fusion_pa_kernel(tc, o1, o2, o3, We1, be1, We2, be2, out):
@@ -32,70 +32,66 @@ def tile_tensor_fusion_pa_kernel(tc, o1, o2, o3, We1, be1, We2, be2, out):
     with ExitStack() as ctx:
         ctx.enter_context(tc.manual_schedule())
         const = ctx.enter_context(tc.tile_pool(name="const", bufs=1))
-        wpools = {}
-        for n in (1, 2, 4):
-            wpools[n] = ctx.enter_context(tc.tile_pool(name="w%d" % n, bufs=W_BUFS[n]))
-        gpool = ctx.enter_context(tc.tile_pool(name="grouped", bufs=3))
-        cpool = ctx.enter_context(tc.tile_pool(name="wcodes", bufs=3))
-        spool = ctx.enter_context(tc.tile_pool(name="fstage", bufs=2))
-        fpool = ctx.enter_context(tc.tile_pool(name="fcodes", bufs=2))
+        wpool = ctx.enter_context(tc.tile_pool(name="wpool", bufs=W_BUFS))
+        gpool = ctx.enter_context(tc.tile_pool(name="grouped", bufs=G_BUFS))
+        cpool = ctx.enter_context(tc.tile_pool(name="wcodes", bufs=4))
+        spool = ctx.enter_context(tc.tile_pool(name="fstage", bufs=STAGE))
+        fpool = ctx.enter_context(tc.tile_pool(name="fcodes", bufs=12))
         hps = ctx.enter_context(tc.psum_pool(name="hps", bufs=1))
         pbps = ctx.enter_context(tc.psum_pool(name="pbps", bufs=2))
         tps = ctx.enter_context(tc.psum_pool(name="tps", bufs=5))
 
-        ident_f = const.tile([P, P], F32, name="ident_f")
-        make_identity(nc, ident_f[:])
-        ident_b = const.tile([P, P], BF16, name="ident_b")
-        make_identity(nc, ident_b[:])
+        starts = []
+        total = 0
+        for n in RANGES:
+            starts.append(total)
+            total += n
+        assert total == ROUNDS
+        tiles = []
+        jobs = []
+        for j, n in enumerate(RANGES):
+            for m in range(4):
+                tiles.append((j, m))
+                for r in range(starts[j], starts[j] + n):
+                    jobs.append((j, m, r))
+        complete_slot = {}
+        for k, job in enumerate(jobs):
+            complete_slot[job[2]] = k // 4
 
         oraw = const.tile([P, 3, DP], BF16, name="oraw")
-        p_all = const.tile([P, 3, DP], BF16, name="p_all")
-        nc.vector.memset(p_all[:], 1.0)
         nc.sync.dma_start(out=oraw[:, 1, 0:31], in_=o2)
         nc.sync.dma_start(out=oraw[:, 2, 0:31], in_=o3)
         nc.sync.dma_start(out=oraw[:, 0, 0:31], in_=o1)
+        ident_b = const.tile([P, P], BF16, name="ident_b")
+        make_identity(nc, ident_b[:])
+        ident_f = const.tile([P, P], F32, name="ident_f")
+        make_identity(nc, ident_f[:])
+        p_all = const.tile([P, 3, DP], BF16, name="p_all")
+        nc.vector.memset(p_all[:], 1.0)
         w2raw = const.tile([P, 2, F], BF16, name="w2raw")
         be1B = const.tile([P, F], BF16, name="be1B")
         be2B = const.tile([P, M], BF16, name="be2B")
 
-        we1v = We1.rearrange("(m p) k -> p m k", p=P)
-        starts = []
-        acc = 0
-        for n in RANGES:
-            starts.append(acc)
-            acc += n
-        assert acc == ROUNDS
-        wtiles = {}
-        state = {"next": 0}
-        range_of_round = []
-        for j, n in enumerate(RANGES):
-            for q in range(n):
-                range_of_round.append(j)
+        wviews = {}
+        st = {"tile": 0, "done": -1, "job": 0, "f": 0, "q": 0, "pend_pb": [], "pend_pg": []}
 
-        def prev_same(j):
-            same = [x for x in range(j) if RANGES[x] == RANGES[j]]
-            nb = W_BUFS[RANGES[j]]
-            if len(same) < nb:
-                return None
-            return same[len(same) - nb]
-
-        def emit_loads(done_round):
-            while state["next"] < len(RANGES):
-                j = state["next"]
-                pj = prev_same(j)
-                if pj is not None and starts[pj] + RANGES[pj] - 1 > done_round:
-                    return
+        def emit_loads():
+            while st["tile"] < len(tiles) and st["tile"] <= st["done"] + W_BUFS:
+                j, m = tiles[st["tile"]]
                 n = RANGES[j]
-                wt = wpools[n].tile([P, 4, n * 1024], BF16, name="wt%d" % n, tag="wt%d" % n)
-                nc.sync.dma_start(out=wt[:], in_=we1v[:, :, starts[j] * 1024:(starts[j] + n) * 1024])
-                wtiles[j] = wt[:].bitcast(F32)
-                if j == 5:
+                wt = wpool.tile([P, n * 1024], BF16, name="wt", tag="wt")
+                nc.sync.dma_start(
+                    out=wt[:],
+                    in_=We1[P * m:P * m + P, starts[j] * 1024:(starts[j] + n) * 1024],
+                )
+                wviews[(j, m)] = wt[:].bitcast(F32)
+                if st["tile"] == 19:
                     nc.sync.dma_start(out=w2raw[:], in_=We2.rearrange("(a p) f -> p a f", p=P))
                     nc.sync.dma_start(out=be1B[:], in_=be1.partition_broadcast(P))
                     nc.sync.dma_start(out=be2B[:], in_=be2.partition_broadcast(P))
-                state["next"] = j + 1
+                st["tile"] += 1
 
-        emit_loads(-1)
+        emit_loads()
 
         nc.vector.tensor_copy(out=p_all[:, :, 0:31], in_=oraw[:, :, 0:31])
         gb = const.tile([P, 1024], F32, name="gb")
@@ -108,14 +104,13 @@ def tile_tensor_fusion_pa_kernel(tc, o1, o2, o3, We1, be1, We2, be2, out):
             )
 
         pbs = {}
+        pgs = {}
 
         def emit_pb(c):
             pb = pbps.tile([P, 4, B], F32, name="pb", tag="pb")
             pbs[c] = pb
             for il in range(4):
                 i = 4 * c + il
-                if i == 31:
-                    continue
                 nc.tensor.matmul(
                     out=pb[:, il, :],
                     lhsT=p_all[:, 0, i:i + 1].to_broadcast([P, P]),
@@ -124,8 +119,22 @@ def tile_tensor_fusion_pa_kernel(tc, o1, o2, o3, We1, be1, We2, be2, out):
                     stop=True,
                 )
 
+        def emit_pg(c):
+            xpg = tps.tile([P, 8, BG], F32, name="xpg", tag="xt")
+            for il in range(8):
+                i = 8 * c + il
+                nc.tensor.matmul(
+                    out=xpg[:, il, :],
+                    lhsT=p_all[:, 0, i:i + 1].to_broadcast([P, P]),
+                    rhs=ident_b[:, BV:B],
+                    start=True,
+                    stop=True,
+                )
+            pg = const.tile([P, 8, BG], BF16, name="pg%d" % c)
+            nc.scalar.copy(out=pg[:], in_=xpg[:])
+            pgs[c] = pg
+
         emit_pb(0)
-        emit_pb(1)
 
         gT = const.tile([P, 1024], F32, name="gT")
         for jh in range(2):
@@ -140,8 +149,12 @@ def tile_tensor_fusion_pa_kernel(tc, o1, o2, o3, We1, be1, We2, be2, out):
                 nc.scalar.copy(out=dst, in_=src)
             else:
                 nc.vector.tensor_copy(out=dst, in_=src)
+        gT4 = gT[:].rearrange("p (j b t) -> p j b t", j=2, t=4)
+        emit_pg(0)
 
         w2g = const.tile([P, 4 * M], BF16, name="w2g", align_bytes=64)
+        w2c = const.tile([P, M], U32, name="w2c", align_bytes=64)
+        w2s = const.tile([P, M], U8, name="w2s", align_bytes=64)
 
         def emit_w2t():
             x2 = tps.tile([P, 2, 4, P], BF16, name="x2", tag="xt")
@@ -153,59 +166,63 @@ def tile_tensor_fusion_pa_kernel(tc, o1, o2, o3, We1, be1, We2, be2, out):
                 in_=x2[:].rearrange("p a t f -> p a f t"),
             )
 
-        w2c = const.tile([P, M], U32, name="w2c", align_bytes=64)
-        w2s = const.tile([P, M], U8, name="w2s", align_bytes=64)
-
         fstages = {}
         fcodes = {}
 
         def emit_fg(i):
-            q, il = i // 4, i % 4
-            if il == 0:
-                fstages[q] = spool.tile([P, 4096], BF16, name="fst", tag="fst", align_bytes=64)
-            dst = fstages[q][:, 1024 * il:1024 * il + 1024]
-            if i == 31:
-                nc.scalar.copy(out=dst, in_=gT[:])
+            if i >= ROUNDS:
                 return
+            fst = spool.tile([P, 1024], BF16, name="fst", tag="fst", align_bytes=64)
+            fstages[i] = fst
+            f4 = fst[:].rearrange("p (j b t) -> p j b t", j=2, t=4)
             nc.vector.tensor_tensor(
-                out=dst.rearrange("p (j b t) -> p j b t", j=2, t=4),
-                in0=gT[:].rearrange("p (j b t) -> p j b t", j=2, t=4),
-                in1=pbs[q][:, il, :].unsqueeze(1).unsqueeze(3).broadcast_to([P, 2, B, 4]),
+                out=f4[:, :, 0:BV, :],
+                in0=gT4[:, :, 0:BV, :],
+                in1=pbs[i // 4][:, i % 4, 0:BV].unsqueeze(1).unsqueeze(3).broadcast_to([P, 2, BV, 4]),
                 op=ALU.mult,
             )
+            nc.gpsimd.tensor_tensor(
+                out=f4[:, :, BV:B, :],
+                in0=gT4[:, :, BV:B, :],
+                in1=pgs[i // 8][:, i % 8, :].unsqueeze(1).unsqueeze(3).broadcast_to([P, 2, BG, 4]),
+                op=ALU.mult,
+            )
+            if (i + 5) % 4 == 0 and 2 <= (i + 5) // 4 < 8:
+                st["pend_pb"] = st["pend_pb"] + [(i + 5) // 4]
+            if i % 8 == 3 and i < 24:
+                st["pend_pg"] = st["pend_pg"] + [(i + 5) // 8]
 
-        def emit_qf(q):
-            fc = fpool.tile([P, 1024], U32, name="fc", tag="fc", align_bytes=64)
-            fs = fpool.tile([P, 1024], U8, name="fs", tag="fs", align_bytes=64)
-            nc.vector.quantize_mx(out=fc[:].bitcast(FP8X4), scales=fs[:], in_=fstages[q][:])
-            fcodes[q] = (fc, fs)
+        def emit_qf(i):
+            fc = fpool.tile([P, 256], U32, name="fc", tag="fc", align_bytes=64)
+            fs = fpool.tile([P, 256], U8, name="fs", tag="fs", align_bytes=64)
+            nc.vector.quantize_mx(out=fc[:].bitcast(FP8X4), scales=fs[:], in_=fstages[i][:])
+            fcodes[i] = (fc, fs)
 
         groupeds = {}
         wcodes = {}
 
-        def emit_t_e(r):
-            j = range_of_round[r]
-            ww = wtiles[j]
+        def emit_job():
+            if st["job"] >= len(jobs):
+                return
+            j, m, r = jobs[st["job"]]
+            st["job"] += 1
+            ww = wviews[(j, m)]
             base = (r - starts[j]) * 512
-            grouped = gpool.tile([P, 4096], BF16, name="grouped", tag="grouped", align_bytes=64)
-            groupeds[r] = grouped
-            gw = grouped[:].bitcast(F32)
+            if m == 0:
+                groupeds[r] = gpool.tile([P, 4096], BF16, name="grouped", tag="grouped", align_bytes=64)
+            gw = groupeds[r][:].bitcast(F32).rearrange("p (j f u) -> p j f u", j=2, u=2)
+            xt = tps.tile([P, 2, 2, P], F32, name="xt", tag="xt")
             for jh in range(2):
-                for h in range(2):
-                    xt = tps.tile([P, 2, 256], F32, name="xt", tag="xt")
-                    for u in range(2):
-                        for mm in range(2):
-                            c0 = base + 256 * jh + 128 * u
-                            nc.tensor.transpose(
-                                out=xt[:, u, 128 * mm:128 * mm + 128],
-                                in_=ww[:, 2 * h + mm, c0:c0 + 128],
-                                identity=ident_f[:],
-                            )
-                    w0 = 1024 * jh + 512 * h
-                    nc.scalar.copy(
-                        out=gw[:, w0:w0 + 512].rearrange("p (f u) -> p f u", u=2),
-                        in_=xt[:].rearrange("p u f -> p f u"),
-                    )
+                for u in range(2):
+                    c0 = base + 256 * jh + 128 * u
+                    nc.tensor.transpose(out=xt[:, jh, u, :], in_=ww[:, c0:c0 + 128], identity=ident_f[:])
+            nc.scalar.copy(
+                out=gw[:, :, P * m:P * m + P, :],
+                in_=xt[:].rearrange("p j u f -> p j f u"),
+            )
+            if st["job"] == len(jobs) or jobs[st["job"]][0:2] != (j, m):
+                st["done"] += 1
+                emit_loads()
 
         def emit_qw(r):
             wc = cpool.tile([P, 1024], U32, name="wc", tag="wc", align_bytes=64)
@@ -217,42 +234,54 @@ def tile_tensor_fusion_pa_kernel(tc, o1, o2, o3, We1, be1, We2, be2, out):
 
         def emit_m(r):
             wc, ws = wcodes[r]
-            fc, fs = fcodes[r // 4]
+            fc, fs = fcodes[r]
             for jh in range(2):
                 g = 2 * r + jh
-                s0 = ((r % 4) * 2 + jh) * 128
                 nc.tensor.matmul_mx(
                     out=hacc[:],
-                    lhsT=fc[:, s0:s0 + 128].bitcast(FP8X4),
-                    lhsT_scale=fs[:, s0:s0 + 128],
+                    lhsT=fc[:, 128 * jh:128 * jh + 128].bitcast(FP8X4),
+                    lhsT_scale=fs[:, 128 * jh:128 * jh + 128],
                     rhs=wc[:, 512 * jh:512 * jh + 512].bitcast(FP8X4),
                     rhs_scale=ws[:, 512 * jh:512 * jh + 512],
                     start=(g == 0),
                     stop=(g == 2 * ROUNDS - 1),
                 )
 
-        for i in range(LEAD):
+        for k in range(4):
+            emit_job()
+        emit_pb(1)
+        for i in range(STAGE):
             emit_fg(i)
-        emit_qf(0)
 
-        for s in range(-2, ROUNDS):
+        for s in range(ROUNDS):
             if s == 12:
                 emit_w2t()
-            if s + 2 < ROUNDS:
-                emit_t_e(s + 2)
-                emit_loads(s + 2)
-            if s < 0:
-                continue
-            emit_qw(s)
+            for k in range(4):
+                emit_job()
+            done_q = []
+            for u in range(2):
+                f_left = st["f"] < ROUNDS
+                q = st["q"]
+                can_q = q < ROUNDS and (complete_slot[q] < s or (not f_left and complete_slot[q] <= s))
+                if (u == 0 and can_q) or not f_left:
+                    emit_qw(q)
+                    done_q.append(q)
+                    st["q"] += 1
+                else:
+                    emit_qf(st["f"])
+                    emit_fg(st["f"] + STAGE)
+                    st["f"] += 1
             if s == 13:
                 nc.vector.quantize_mx(out=w2c[:].bitcast(FP8X4), scales=w2s[:], in_=w2g[:])
-            if s >= 2 and (s + 2) % 4 == 0 and (s + 2) // 4 < 8:
-                emit_qf((s + 2) // 4)
-            if s + LEAD < ROUNDS:
-                emit_fg(s + LEAD)
-            emit_m(s)
-            if s % 4 == 0 and s // 4 + 2 < 8:
-                emit_pb(s // 4 + 2)
+            for q in done_q:
+                emit_m(q)
+            for c in st["pend_pb"]:
+                emit_pb(c)
+            st["pend_pb"] = []
+            for c in st["pend_pg"]:
+                emit_pg(c)
+            st["pend_pg"] = []
+        assert st["q"] == ROUNDS and st["f"] == ROUNDS
 
         hs = const.tile([P, F], BF16, name="hs")
         nc.vector.tensor_tensor(out=hs[:], in0=hacc[:], in1=be1B[:], op=ALU.add)

@@ -258,19 +258,31 @@ def tile_tensor_fusion_pa_kernel(tc, o1, o2, o3, We1, be1, We2, be2, out):
                 emit_w2t()
             for k in range(4):
                 emit_job()
-            done_q = []
+            units = []
+            nq = st["q"]
+            nf = st["f"]
             for u in range(2):
-                f_left = st["f"] < ROUNDS
-                q = st["q"]
-                can_q = q < ROUNDS and (complete_slot[q] < s or (not f_left and complete_slot[q] <= s))
+                f_left = nf < ROUNDS
+                can_q = nq < ROUNDS and (complete_slot[nq] < s or (not f_left and complete_slot[nq] <= s))
                 if (u == 0 and can_q) or not f_left:
-                    emit_qw(q)
-                    done_q.append(q)
-                    st["q"] += 1
+                    units.append(("q", nq))
+                    nq += 1
                 else:
-                    emit_qf(st["f"])
-                    emit_fg(st["f"] + STAGE)
-                    st["f"] += 1
+                    units.append(("f", nf))
+                    nf += 1
+            st["q"] = nq
+            st["f"] = nf
+            done_q = []
+            for kind, x in units:
+                if kind == "f":
+                    emit_qf(x)
+            for kind, x in units:
+                if kind == "q":
+                    emit_qw(x)
+                    done_q.append(x)
+            for kind, x in units:
+                if kind == "f":
+                    emit_fg(x + STAGE)
             if s == 13:
                 nc.vector.quantize_mx(out=w2c[:].bitcast(FP8X4), scales=w2s[:], in_=w2g[:])
             for q in done_q:

@@ -25,6 +25,7 @@ G_BUFS = 9
 STAGE = 2
 BG = 32
 BV = B - BG
+WARM = 4
 
 
 def tile_tensor_fusion_pa_kernel(tc, o1, o2, o3, We1, be1, We2, be2, out):
@@ -66,8 +67,17 @@ def tile_tensor_fusion_pa_kernel(tc, o1, o2, o3, We1, be1, We2, be2, out):
         make_identity(nc, ident_b[:])
         ident_f = const.tile([P, P], F32, name="ident_f")
         make_identity(nc, ident_f[:])
+        dz = const.tile([P, F], BF16, name="dz")
+        nc.vector.memset(dz[:], 0.0)
         p_all = const.tile([P, 3, DP], BF16, name="p_all")
         nc.vector.memset(p_all[:], 1.0)
+
+        def emit_idle():
+            xd = tps.tile([P, F], F32, name="xd", tag="xt")
+            nc.tensor.matmul(out=xd[:], lhsT=dz[:, 0:P], rhs=dz[:], start=True, stop=True)
+
+        for k in range(WARM):
+            emit_idle()
         w2raw = const.tile([P, 2, F], BF16, name="w2raw")
         be1B = const.tile([P, F], BF16, name="be1B")
         be2B = const.tile([P, M], BF16, name="be2B")
@@ -256,8 +266,11 @@ def tile_tensor_fusion_pa_kernel(tc, o1, o2, o3, We1, be1, We2, be2, out):
         for s in range(ROUNDS):
             if s == 12:
                 emit_w2t()
+            no_pass = st["f"] < ROUNDS and not (st["q"] < ROUNDS and complete_slot[st["q"]] < s)
             for k in range(4):
                 emit_job()
+                if no_pass and k % 2 == 1:
+                    emit_idle()
             units = []
             nq = st["q"]
             nf = st["f"]

@@ -25,7 +25,6 @@ G_BUFS = 9
 STAGE = 2
 BG = 32
 BV = B - BG
-WARM = 4
 
 
 def tile_tensor_fusion_pa_kernel(tc, o1, o2, o3, We1, be1, We2, be2, out):
@@ -35,9 +34,9 @@ def tile_tensor_fusion_pa_kernel(tc, o1, o2, o3, We1, be1, We2, be2, out):
         const = ctx.enter_context(tc.tile_pool(name="const", bufs=1))
         wpool = ctx.enter_context(tc.tile_pool(name="wpool", bufs=W_BUFS))
         gpool = ctx.enter_context(tc.tile_pool(name="grouped", bufs=G_BUFS))
-        cpool = ctx.enter_context(tc.tile_pool(name="wcodes", bufs=4))
+        cpool = ctx.enter_context(tc.tile_pool(name="wcodes", bufs=6))
         spool = ctx.enter_context(tc.tile_pool(name="fstage", bufs=STAGE))
-        fpool = ctx.enter_context(tc.tile_pool(name="fcodes", bufs=12))
+        fpool = ctx.enter_context(tc.tile_pool(name="fcodes", bufs=14))
         hps = ctx.enter_context(tc.psum_pool(name="hps", bufs=1))
         pbps = ctx.enter_context(tc.psum_pool(name="pbps", bufs=2))
         tps = ctx.enter_context(tc.psum_pool(name="tps", bufs=5))
@@ -55,6 +54,7 @@ def tile_tensor_fusion_pa_kernel(tc, o1, o2, o3, We1, be1, We2, be2, out):
                 tiles.append((j, m))
                 for r in range(starts[j], starts[j] + n):
                     jobs.append((j, m, r))
+        LAST = ROUNDS - 1
         complete_slot = {}
         for k, job in enumerate(jobs):
             complete_slot[job[2]] = k // 4
@@ -67,23 +67,14 @@ def tile_tensor_fusion_pa_kernel(tc, o1, o2, o3, We1, be1, We2, be2, out):
         make_identity(nc, ident_b[:])
         ident_f = const.tile([P, P], F32, name="ident_f")
         make_identity(nc, ident_f[:])
-        dz = const.tile([P, F], BF16, name="dz")
-        nc.vector.memset(dz[:], 0.0)
         p_all = const.tile([P, 3, DP], BF16, name="p_all")
         nc.vector.memset(p_all[:], 1.0)
-
-        def emit_idle():
-            xd = tps.tile([P, F], F32, name="xd", tag="xt")
-            nc.tensor.matmul(out=xd[:], lhsT=dz[:, 0:P], rhs=dz[:], start=True, stop=True)
-
-        for k in range(WARM):
-            emit_idle()
         w2raw = const.tile([P, 2, F], BF16, name="w2raw")
         be1B = const.tile([P, F], BF16, name="be1B")
         be2B = const.tile([P, M], BF16, name="be2B")
 
         wviews = {}
-        st = {"tile": 0, "done": -1, "job": 0, "f": 0, "q": 0, "pend_pb": [], "pend_pg": []}
+        st = {"tile": 0, "done": -1, "job": 0, "f": 0, "q": 0, "pend_pb": [], "pend_pg": [], "ripe": [], "held": False}
 
         def emit_loads():
             while st["tile"] < len(tiles) and st["tile"] <= st["done"] + W_BUFS:
@@ -216,12 +207,23 @@ def tile_tensor_fusion_pa_kernel(tc, o1, o2, o3, We1, be1, We2, be2, out):
                 return
             j, m, r = jobs[st["job"]]
             st["job"] += 1
-            ww = wviews[(j, m)]
             base = (r - starts[j]) * 512
             if m == 0:
                 groupeds[r] = gpool.tile([P, 4096], BF16, name="grouped", tag="grouped", align_bytes=64)
             gw = groupeds[r][:].bitcast(F32).rearrange("p (j f u) -> p j f u", j=2, u=2)
             xt = tps.tile([P, 2, 2, P], F32, name="xt", tag="xt")
+            if r == LAST:
+                jh, h = m // 2, m % 2
+                for u in range(2):
+                    for a in range(2):
+                        c0 = base + 256 * jh + 128 * u
+                        nc.tensor.transpose(out=xt[:, u, a, :], in_=wviews[(j, 2 * h + a)][:, c0:c0 + 128], identity=ident_f[:])
+                nc.scalar.copy(
+                    out=gw[:, jh, 256 * h:256 * h + 256, :],
+                    in_=xt[:].rearrange("p u a f -> p (a f) u"),
+                )
+                return
+            ww = wviews[(j, m)]
             for jh in range(2):
                 for u in range(2):
                     c0 = base + 256 * jh + 128 * u
@@ -235,24 +237,30 @@ def tile_tensor_fusion_pa_kernel(tc, o1, o2, o3, We1, be1, We2, be2, out):
                 emit_loads()
 
         def emit_qw(r):
-            wc = cpool.tile([P, 1024], U32, name="wc", tag="wc", align_bytes=64)
-            ws = cpool.tile([P, 1024], U8, name="ws", tag="ws", align_bytes=64)
-            nc.vector.quantize_mx(out=wc[:].bitcast(FP8X4), scales=ws[:], in_=groupeds[r][:])
-            wcodes[r] = (wc, ws)
+            widths = [1024] if r != LAST else [512, 512]
+            g = 2 * r
+            for wd in widths:
+                wc = cpool.tile([P, wd], U32, name="wc", tag="wc", align_bytes=64)
+                ws = cpool.tile([P, wd], U8, name="ws", tag="ws", align_bytes=64)
+                lo = (g - 2 * r) * 2048
+                nc.vector.quantize_mx(out=wc[:].bitcast(FP8X4), scales=ws[:], in_=groupeds[r][:, lo:lo + 4 * wd])
+                for x in range(wd // 512):
+                    wcodes[g] = (wc[:, 512 * x:512 * x + 512], ws[:, 512 * x:512 * x + 512])
+                    g += 1
 
         hacc = hps.tile([P, F], F32, name="hacc")
 
         def emit_m(r):
-            wc, ws = wcodes[r]
             fc, fs = fcodes[r]
             for jh in range(2):
                 g = 2 * r + jh
+                wc, ws = wcodes[g]
                 nc.tensor.matmul_mx(
                     out=hacc[:],
                     lhsT=fc[:, 128 * jh:128 * jh + 128].bitcast(FP8X4),
                     lhsT_scale=fs[:, 128 * jh:128 * jh + 128],
-                    rhs=wc[:, 512 * jh:512 * jh + 512].bitcast(FP8X4),
-                    rhs_scale=ws[:, 512 * jh:512 * jh + 512],
+                    rhs=wc.bitcast(FP8X4),
+                    rhs_scale=ws,
                     start=(g == 0),
                     stop=(g == 2 * ROUNDS - 1),
                 )
@@ -266,11 +274,8 @@ def tile_tensor_fusion_pa_kernel(tc, o1, o2, o3, We1, be1, We2, be2, out):
         for s in range(ROUNDS):
             if s == 12:
                 emit_w2t()
-            no_pass = st["f"] < ROUNDS and not (st["q"] < ROUNDS and complete_slot[st["q"]] < s)
             for k in range(4):
                 emit_job()
-                if no_pass and k % 2 == 1:
-                    emit_idle()
             units = []
             nq = st["q"]
             nf = st["f"]
@@ -298,14 +303,26 @@ def tile_tensor_fusion_pa_kernel(tc, o1, o2, o3, We1, be1, We2, be2, out):
                     emit_fg(x + STAGE)
             if s == 13:
                 nc.vector.quantize_mx(out=w2c[:].bitcast(FP8X4), scales=w2s[:], in_=w2g[:])
-            for q in done_q:
-                emit_m(q)
-            for c in st["pend_pb"]:
-                emit_pb(c)
-            st["pend_pb"] = []
-            for c in st["pend_pg"]:
-                emit_pg(c)
-            st["pend_pg"] = []
+            ripe = st["ripe"]
+            if s == ROUNDS - 1:
+                ripe = ripe + done_q
+                done_q = []
+            run = len(ripe) >= 2 or s == ROUNDS - 1
+            if run:
+                for q in ripe:
+                    emit_m(q)
+                ripe = []
+            st["ripe"] = ripe + done_q
+            if run or st["held"] or s < 4:
+                for c in st["pend_pb"]:
+                    emit_pb(c)
+                st["pend_pb"] = []
+                for c in st["pend_pg"]:
+                    emit_pg(c)
+                st["pend_pg"] = []
+                st["held"] = False
+            else:
+                st["held"] = len(st["pend_pb"]) + len(st["pend_pg"]) > 0
         assert st["q"] == ROUNDS and st["f"] == ROUNDS
 
         hs = const.tile([P, F], BF16, name="hs")

@@ -19,12 +19,13 @@ FUSED = DP * DP * DP
 ROUNDS = 32
 FLOPS = 2 * B * FUSED * F + 2 * B * F * M
 
-RANGES = [2, 2, 4, 4, 4, 4, 4, 4, 2, 1, 1]
+RANGES = [1, 1, 2, 4, 4, 4, 4, 4, 4, 2, 1, 1]
 W_BUFS = 8
 G_BUFS = 9
 STAGE = 2
 BG = 32
 BV = B - BG
+WARM = 4
 
 
 def tile_tensor_fusion_pa_kernel(tc, o1, o2, o3, We1, be1, We2, be2, out):
@@ -67,14 +68,19 @@ def tile_tensor_fusion_pa_kernel(tc, o1, o2, o3, We1, be1, We2, be2, out):
         make_identity(nc, ident_b[:])
         ident_f = const.tile([P, P], F32, name="ident_f")
         make_identity(nc, ident_f[:])
+        dz = const.tile([P, F], BF16, name="dz")
+        nc.vector.memset(dz[:], 0.0)
         p_all = const.tile([P, 3, DP], BF16, name="p_all")
         nc.vector.memset(p_all[:], 1.0)
+        for k in range(WARM):
+            xd = tps.tile([P, F], F32, name="xd", tag="xt")
+            nc.tensor.matmul(out=xd[:], lhsT=dz[:, 0:P], rhs=dz[:], start=True, stop=True)
         w2raw = const.tile([P, 2, F], BF16, name="w2raw")
         be1B = const.tile([P, F], BF16, name="be1B")
         be2B = const.tile([P, M], BF16, name="be2B")
 
         wviews = {}
-        st = {"tile": 0, "done": -1, "job": 0, "f": 0, "q": 0, "pend_pb": [], "pend_pg": [], "ripe": [], "held": False}
+        st = {"tile": 0, "done": -1, "job": 0, "f": 0, "q": 0, "pend_pb": [], "pend_pg": []}
 
         def emit_loads():
             while st["tile"] < len(tiles) and st["tile"] <= st["done"] + W_BUFS:
@@ -86,7 +92,7 @@ def tile_tensor_fusion_pa_kernel(tc, o1, o2, o3, We1, be1, We2, be2, out):
                     in_=We1[P * m:P * m + P, starts[j] * 1024:(starts[j] + n) * 1024],
                 )
                 wviews[(j, m)] = wt[:].bitcast(F32)
-                if st["tile"] == 19:
+                if st["tile"] == 23:
                     nc.sync.dma_start(out=w2raw[:], in_=We2.rearrange("(a p) f -> p a f", p=P))
                     nc.sync.dma_start(out=be1B[:], in_=be1.partition_broadcast(P))
                     nc.sync.dma_start(out=be2B[:], in_=be2.partition_broadcast(P))
@@ -96,11 +102,11 @@ def tile_tensor_fusion_pa_kernel(tc, o1, o2, o3, We1, be1, We2, be2, out):
 
         nc.vector.tensor_copy(out=p_all[:, :, 0:31], in_=oraw[:, :, 0:31])
         gb = const.tile([P, 1024], F32, name="gb")
-        for jh in range(2):
+        for w in range(4):
             nc.vector.tensor_tensor(
-                out=gb[:, 512 * jh:512 * jh + 512].rearrange("p (j k) -> p j k", j=16),
-                in0=p_all[:, 1, 16 * jh:16 * jh + 16].unsqueeze(2).broadcast_to([P, 16, DP]),
-                in1=p_all[:, 2, :].unsqueeze(1).broadcast_to([P, 16, DP]),
+                out=gb[:, 256 * w:256 * w + 256].rearrange("p (e j k) -> p e j k", e=2, j=8),
+                in0=p_all[:, 1, 8 * w:8 * w + 8].unsqueeze(1).unsqueeze(3).broadcast_to([P, 2, 8, 16]),
+                in1=p_all[:, 2, :].rearrange("p (k e) -> p e k", e=2).unsqueeze(2).broadcast_to([P, 2, 8, 16]),
                 op=ALU.mult,
             )
 
@@ -135,23 +141,18 @@ def tile_tensor_fusion_pa_kernel(tc, o1, o2, o3, We1, be1, We2, be2, out):
             nc.scalar.copy(out=pg[:], in_=xpg[:])
             pgs[c] = pg
 
-        emit_pb(0)
-
         gT = const.tile([P, 1024], F32, name="gT")
-        for jh in range(2):
+        gT4 = gT[:].rearrange("p (j b t) -> p j b t", j=2, t=4)
+
+        def emit_gt(jh):
             xg = tps.tile([P, 4, B], F32, name="xg", tag="xt")
             for t in range(4):
-                u, e = t // 2, t % 2
-                c0 = 512 * jh + 256 * u + e
-                nc.tensor.transpose(out=xg[:, t, :], in_=gb[:, c0:c0 + 255:2], identity=ident_f[:])
-            dst = gT[:, 512 * jh:512 * jh + 512].rearrange("p (b t) -> p b t", t=4)
-            src = xg[:].rearrange("p t b -> p b t")
-            if jh == 0:
-                nc.scalar.copy(out=dst, in_=src)
-            else:
-                nc.vector.tensor_copy(out=dst, in_=src)
-        gT4 = gT[:].rearrange("p (j b t) -> p j b t", j=2, t=4)
-        emit_pg(0)
+                c0 = 512 * jh + 128 * t
+                nc.tensor.transpose(out=xg[:, t, :], in_=gb[:, c0:c0 + 128], identity=ident_f[:])
+            nc.vector.tensor_copy(
+                out=gT[:, 512 * jh:512 * jh + 512].rearrange("p (b t) -> p b t", t=4),
+                in_=xg[:].rearrange("p t b -> p b t"),
+            )
 
         w2g = const.tile([P, 4 * M], BF16, name="w2g", align_bytes=64)
         w2c = const.tile([P, M], U32, name="w2c", align_bytes=64)
@@ -265,7 +266,12 @@ def tile_tensor_fusion_pa_kernel(tc, o1, o2, o3, We1, be1, We2, be2, out):
                     stop=(g == 2 * ROUNDS - 1),
                 )
 
-        for k in range(4):
+        emit_pb(0)
+        emit_gt(0)
+        emit_job()
+        emit_gt(1)
+        emit_pg(0)
+        for k in range(3):
             emit_job()
         emit_pb(1)
         for i in range(STAGE):
@@ -303,26 +309,14 @@ def tile_tensor_fusion_pa_kernel(tc, o1, o2, o3, We1, be1, We2, be2, out):
                     emit_fg(x + STAGE)
             if s == 13:
                 nc.vector.quantize_mx(out=w2c[:].bitcast(FP8X4), scales=w2s[:], in_=w2g[:])
-            ripe = st["ripe"]
-            if s == ROUNDS - 1:
-                ripe = ripe + done_q
-                done_q = []
-            run = len(ripe) >= 2 or s == ROUNDS - 1
-            if run:
-                for q in ripe:
-                    emit_m(q)
-                ripe = []
-            st["ripe"] = ripe + done_q
-            if run or st["held"] or s < 4:
-                for c in st["pend_pb"]:
-                    emit_pb(c)
-                st["pend_pb"] = []
-                for c in st["pend_pg"]:
-                    emit_pg(c)
-                st["pend_pg"] = []
-                st["held"] = False
-            else:
-                st["held"] = len(st["pend_pb"]) + len(st["pend_pg"]) > 0
+            for q in done_q:
+                emit_m(q)
+            for c in st["pend_pb"]:
+                emit_pb(c)
+            st["pend_pb"] = []
+            for c in st["pend_pg"]:
+                emit_pg(c)
+            st["pend_pg"] = []
         assert st["q"] == ROUNDS and st["f"] == ROUNDS
 
         hs = const.tile([P, F], BF16, name="hs")

@@ -23,7 +23,8 @@ RANGES = [1, 1, 2, 4, 4, 4, 4, 4, 4, 2, 1, 1]
 W_BUFS = 8
 G_BUFS = 9
 STAGE = 2
-BG = 32
+BG = 40
+PGW = 64
 BV = B - BG
 WARM = 4
 
@@ -127,18 +128,18 @@ def tile_tensor_fusion_pa_kernel(tc, o1, o2, o3, We1, be1, We2, be2, out):
                 )
 
         def emit_pg(c):
-            xpg = tps.tile([P, 8, BG], F32, name="xpg", tag="xt")
+            xpg = tps.tile([P, 8, PGW], F32, name="xpg", tag="xt")
             for il in range(8):
                 i = 8 * c + il
                 nc.tensor.matmul(
                     out=xpg[:, il, :],
                     lhsT=p_all[:, 0, i:i + 1].to_broadcast([P, P]),
-                    rhs=ident_b[:, BV:B],
+                    rhs=ident_b[:, B - PGW:B],
                     start=True,
                     stop=True,
                 )
             pg = const.tile([P, 8, BG], BF16, name="pg%d" % c)
-            nc.scalar.copy(out=pg[:], in_=xpg[:])
+            nc.scalar.copy(out=pg[:], in_=xpg[:, :, PGW - BG:PGW])
             pgs[c] = pg
 
         gT = const.tile([P, 1024], F32, name="gT")

@@ -23,8 +23,7 @@ RANGES = [1, 1, 2, 4, 4, 4, 4, 4, 4, 2, 1, 1]
 W_BUFS = 8
 G_BUFS = 9
 STAGE = 2
-BG = 40
-PGW = 64
+BG = 32
 BV = B - BG
 WARM = 4
 
@@ -103,11 +102,11 @@ def tile_tensor_fusion_pa_kernel(tc, o1, o2, o3, We1, be1, We2, be2, out):
 
         nc.vector.tensor_copy(out=p_all[:, :, 0:31], in_=oraw[:, :, 0:31])
         gb = const.tile([P, 1024], F32, name="gb")
-        for w in range(4):
+        for jh in range(2):
             nc.vector.tensor_tensor(
-                out=gb[:, 256 * w:256 * w + 256].rearrange("p (e j k) -> p e j k", e=2, j=8),
-                in0=p_all[:, 1, 8 * w:8 * w + 8].unsqueeze(1).unsqueeze(3).broadcast_to([P, 2, 8, 16]),
-                in1=p_all[:, 2, :].rearrange("p (k e) -> p e k", e=2).unsqueeze(2).broadcast_to([P, 2, 8, 16]),
+                out=gb[:, 512 * jh:512 * jh + 512].rearrange("p (t j k) -> p t j k", t=4, j=16),
+                in0=p_all[:, 1, 16 * jh:16 * jh + 16].unsqueeze(1).unsqueeze(3).broadcast_to([P, 4, 16, 8]),
+                in1=p_all[:, 2, :].rearrange("p (k t) -> p t k", t=4).unsqueeze(2).broadcast_to([P, 4, 16, 8]),
                 op=ALU.mult,
             )
 
@@ -128,18 +127,18 @@ def tile_tensor_fusion_pa_kernel(tc, o1, o2, o3, We1, be1, We2, be2, out):
                 )
 
         def emit_pg(c):
-            xpg = tps.tile([P, 8, PGW], F32, name="xpg", tag="xt")
+            xpg = tps.tile([P, 8, BG], F32, name="xpg", tag="xt")
             for il in range(8):
                 i = 8 * c + il
                 nc.tensor.matmul(
                     out=xpg[:, il, :],
                     lhsT=p_all[:, 0, i:i + 1].to_broadcast([P, P]),
-                    rhs=ident_b[:, B - PGW:B],
+                    rhs=ident_b[:, BV:B],
                     start=True,
                     stop=True,
                 )
             pg = const.tile([P, 8, BG], BF16, name="pg%d" % c)
-            nc.scalar.copy(out=pg[:], in_=xpg[:, :, PGW - BG:PGW])
+            nc.scalar.copy(out=pg[:], in_=xpg[:])
             pgs[c] = pg
 
         gT = const.tile([P, 1024], F32, name="gT")
@@ -218,8 +217,8 @@ def tile_tensor_fusion_pa_kernel(tc, o1, o2, o3, We1, be1, We2, be2, out):
                 jh, h = m // 2, m % 2
                 for u in range(2):
                     for a in range(2):
-                        c0 = base + 256 * jh + 128 * u
-                        nc.tensor.transpose(out=xt[:, u, a, :], in_=wviews[(j, 2 * h + a)][:, c0:c0 + 128], identity=ident_f[:])
+                        c0 = base + 256 * jh
+                        nc.tensor.transpose(out=xt[:, u, a, :], in_=wviews[(j, 2 * h + a)][:, c0 + u:c0 + 256:2], identity=ident_f[:])
                 nc.scalar.copy(
                     out=gw[:, jh, 256 * h:256 * h + 256, :],
                     in_=xt[:].rearrange("p u a f -> p (a f) u"),
@@ -228,8 +227,8 @@ def tile_tensor_fusion_pa_kernel(tc, o1, o2, o3, We1, be1, We2, be2, out):
             ww = wviews[(j, m)]
             for jh in range(2):
                 for u in range(2):
-                    c0 = base + 256 * jh + 128 * u
-                    nc.tensor.transpose(out=xt[:, jh, u, :], in_=ww[:, c0:c0 + 128], identity=ident_f[:])
+                    c0 = base + 256 * jh
+                    nc.tensor.transpose(out=xt[:, jh, u, :], in_=ww[:, c0 + u:c0 + 256:2], identity=ident_f[:])
             nc.scalar.copy(
                 out=gw[:, :, P * m:P * m + P, :],
                 in_=xt[:].rearrange("p j u f -> p j f u"),

@@ -87,10 +87,17 @@ def tile_tensor_fusion_pa_kernel(tc, o1, o2, o3, We1, be1, We2, be2, out):
                 j, m = tiles[st["tile"]]
                 n = RANGES[j]
                 wt = wpool.tile([P, n * 1024], BF16, name="wt", tag="wt")
-                nc.sync.dma_start(
-                    out=wt[:],
-                    in_=We1[P * m:P * m + P, starts[j] * 1024:(starts[j] + n) * 1024],
-                )
+                if n == 1:
+                    q, h = starts[j] // 2, starts[j] % 2
+                    nc.sync.dma_start(
+                        out=wt[:].rearrange("p (u c) -> p u c", u=2),
+                        in_=We1[P * m:P * m + P, 2048 * q:2048 * q + 2048].rearrange("r (u c) -> r u c", u=2)[:, :, 512 * h:512 * h + 512],
+                    )
+                else:
+                    nc.sync.dma_start(
+                        out=wt[:],
+                        in_=We1[P * m:P * m + P, starts[j] * 1024:(starts[j] + n) * 1024],
+                    )
                 wviews[(j, m)] = wt[:].bitcast(F32)
                 if st["tile"] == 23:
                     nc.sync.dma_start(out=w2raw[:], in_=We2.rearrange("(a p) f -> p a f", p=P))
@@ -102,11 +109,11 @@ def tile_tensor_fusion_pa_kernel(tc, o1, o2, o3, We1, be1, We2, be2, out):
 
         nc.vector.tensor_copy(out=p_all[:, :, 0:31], in_=oraw[:, :, 0:31])
         gb = const.tile([P, 1024], F32, name="gb")
-        for jh in range(2):
+        for w in range(4):
             nc.vector.tensor_tensor(
-                out=gb[:, 512 * jh:512 * jh + 512].rearrange("p (t j k) -> p t j k", t=4, j=16),
-                in0=p_all[:, 1, 16 * jh:16 * jh + 16].unsqueeze(1).unsqueeze(3).broadcast_to([P, 4, 16, 8]),
-                in1=p_all[:, 2, :].rearrange("p (k t) -> p t k", t=4).unsqueeze(2).broadcast_to([P, 4, 16, 8]),
+                out=gb[:, 256 * w:256 * w + 256].rearrange("p (e j k) -> p e j k", e=2, j=8),
+                in0=p_all[:, 1, 8 * w:8 * w + 8].unsqueeze(1).unsqueeze(3).broadcast_to([P, 2, 8, 16]),
+                in1=p_all[:, 2, :].rearrange("p (k e) -> p e k", e=2).unsqueeze(2).broadcast_to([P, 2, 8, 16]),
                 op=ALU.mult,
             )
 
@@ -114,12 +121,12 @@ def tile_tensor_fusion_pa_kernel(tc, o1, o2, o3, We1, be1, We2, be2, out):
         pgs = {}
 
         def emit_pb(c):
-            pb = pbps.tile([P, 4, B], F32, name="pb", tag="pb")
+            pb = pbps.tile([P, 2, 2 * B], F32, name="pb", tag="pb")
             pbs[c] = pb
             for il in range(4):
                 i = 4 * c + il
                 nc.tensor.matmul(
-                    out=pb[:, il, :],
+                    out=pb[:, il // 2, il % 2:2 * B:2],
                     lhsT=p_all[:, 0, i:i + 1].to_broadcast([P, P]),
                     rhs=ident_b[:],
                     start=True,
@@ -127,32 +134,34 @@ def tile_tensor_fusion_pa_kernel(tc, o1, o2, o3, We1, be1, We2, be2, out):
                 )
 
         def emit_pg(c):
-            xpg = tps.tile([P, 8, BG], F32, name="xpg", tag="xt")
+            xpg = tps.tile([P, 4, 2 * BG], F32, name="xpg", tag="xt")
             for il in range(8):
                 i = 8 * c + il
                 nc.tensor.matmul(
-                    out=xpg[:, il, :],
+                    out=xpg[:, il // 2, il % 2:2 * BG:2],
                     lhsT=p_all[:, 0, i:i + 1].to_broadcast([P, P]),
                     rhs=ident_b[:, BV:B],
                     start=True,
                     stop=True,
                 )
-            pg = const.tile([P, 8, BG], BF16, name="pg%d" % c)
+            pg = const.tile([P, 4, 2 * BG], BF16, name="pg%d" % c)
             nc.scalar.copy(out=pg[:], in_=xpg[:])
             pgs[c] = pg
 
-        gT = const.tile([P, 1024], F32, name="gT")
-        gT4 = gT[:].rearrange("p (j b t) -> p j b t", j=2, t=4)
+        gT = const.tile([P, 2048], F32, name="gT")
+        gT4 = gT[:].rearrange("p (w n e) -> p w n e", w=4, e=2)
 
         def emit_gt(jh):
             xg = tps.tile([P, 4, B], F32, name="xg", tag="xt")
             for t in range(4):
                 c0 = 512 * jh + 128 * t
                 nc.tensor.transpose(out=xg[:, t, :], in_=gb[:, c0:c0 + 128], identity=ident_f[:])
-            nc.vector.tensor_copy(
-                out=gT[:, 512 * jh:512 * jh + 512].rearrange("p (b t) -> p b t", t=4),
-                in_=xg[:].rearrange("p t b -> p b t"),
-            )
+            for wl in range(2):
+                w = 2 * jh + wl
+                nc.vector.tensor_copy(
+                    out=gT[:, 512 * w:512 * w + 512].rearrange("p (b u e) -> p b u e", u=2, e=2),
+                    in_=xg[:, 2 * wl:2 * wl + 2, :].rearrange("p e b -> p b e").unsqueeze(2).broadcast_to([P, B, 2, 2]),
+                )
 
         w2g = const.tile([P, 4 * M], BF16, name="w2g", align_bytes=64)
         w2c = const.tile([P, M], U32, name="w2c", align_bytes=64)
@@ -176,17 +185,18 @@ def tile_tensor_fusion_pa_kernel(tc, o1, o2, o3, We1, be1, We2, be2, out):
                 return
             fst = spool.tile([P, 1024], BF16, name="fst", tag="fst", align_bytes=64)
             fstages[i] = fst
-            f4 = fst[:].rearrange("p (j b t) -> p j b t", j=2, t=4)
+            f4 = fst[:].rearrange("p (j n e) -> p j n e", j=2, e=2)
+            q, h = i // 2, i % 2
             nc.vector.tensor_tensor(
-                out=f4[:, :, 0:BV, :],
-                in0=gT4[:, :, 0:BV, :],
-                in1=pbs[i // 4][:, i % 4, 0:BV].unsqueeze(1).unsqueeze(3).broadcast_to([P, 2, BV, 4]),
+                out=f4[:, :, 0:2 * BV, :],
+                in0=gT4[:, 2 * h:2 * h + 2, 0:2 * BV, :],
+                in1=pbs[q // 2][:, q % 2, 0:2 * BV].unsqueeze(1).unsqueeze(3).broadcast_to([P, 2, 2 * BV, 2]),
                 op=ALU.mult,
             )
             nc.gpsimd.tensor_tensor(
-                out=f4[:, :, BV:B, :],
-                in0=gT4[:, :, BV:B, :],
-                in1=pgs[i // 8][:, i % 8, :].unsqueeze(1).unsqueeze(3).broadcast_to([P, 2, BG, 4]),
+                out=f4[:, :, 2 * BV:2 * B, :],
+                in0=gT4[:, 2 * h:2 * h + 2, 2 * BV:2 * B, :],
+                in1=pgs[q // 4][:, q % 4, :].unsqueeze(1).unsqueeze(3).broadcast_to([P, 2, 2 * BG, 2]),
                 op=ALU.mult,
             )
             if (i + 5) % 4 == 0 and 2 <= (i + 5) // 4 < 8:
@@ -208,7 +218,10 @@ def tile_tensor_fusion_pa_kernel(tc, o1, o2, o3, We1, be1, We2, be2, out):
                 return
             j, m, r = jobs[st["job"]]
             st["job"] += 1
-            base = (r - starts[j]) * 512
+            if RANGES[j] == 1:
+                c00, ustep = 0, 256
+            else:
+                c00, ustep = (r // 2 * 2 - starts[j]) * 512 + 256 * (r % 2), 512
             if m == 0:
                 groupeds[r] = gpool.tile([P, 4096], BF16, name="grouped", tag="grouped", align_bytes=64)
             gw = groupeds[r][:].bitcast(F32).rearrange("p (j f u) -> p j f u", j=2, u=2)
@@ -217,8 +230,8 @@ def tile_tensor_fusion_pa_kernel(tc, o1, o2, o3, We1, be1, We2, be2, out):
                 jh, h = m // 2, m % 2
                 for u in range(2):
                     for a in range(2):
-                        c0 = base + 256 * jh
-                        nc.tensor.transpose(out=xt[:, u, a, :], in_=wviews[(j, 2 * h + a)][:, c0 + u:c0 + 256:2], identity=ident_f[:])
+                        c0 = c00 + ustep * u + 128 * jh
+                        nc.tensor.transpose(out=xt[:, u, a, :], in_=wviews[(j, 2 * h + a)][:, c0:c0 + 128], identity=ident_f[:])
                 nc.scalar.copy(
                     out=gw[:, jh, 256 * h:256 * h + 256, :],
                     in_=xt[:].rearrange("p u a f -> p (a f) u"),
@@ -227,8 +240,8 @@ def tile_tensor_fusion_pa_kernel(tc, o1, o2, o3, We1, be1, We2, be2, out):
             ww = wviews[(j, m)]
             for jh in range(2):
                 for u in range(2):
-                    c0 = base + 256 * jh
-                    nc.tensor.transpose(out=xt[:, jh, u, :], in_=ww[:, c0 + u:c0 + 256:2], identity=ident_f[:])
+                    c0 = c00 + ustep * u + 128 * jh
+                    nc.tensor.transpose(out=xt[:, jh, u, :], in_=ww[:, c0:c0 + 128], identity=ident_f[:])
             nc.scalar.copy(
                 out=gw[:, :, P * m:P * m + P, :],
                 in_=xt[:].rearrange("p j u f -> p j f u"),

@@ -16,16 +16,19 @@ DP = 32
 F = 512
 M = 256
 FUSED = DP * DP * DP
-ROUNDS = 32
 FLOPS = 2 * B * FUSED * F + 2 * B * F * M
 
+ROUNDS = 32
+LAST = ROUNDS - 1
 RANGES = [1, 1, 2, 4, 4, 4, 4, 4, 4, 2, 1, 1]
 W_BUFS = 8
 G_BUFS = 9
 STAGE = 2
-BG = 32
+BG = 40
 BV = B - BG
 WARM = 4
+PLAG = 2
+MLAG = 2
 
 
 def tile_tensor_fusion_pa_kernel(tc, o1, o2, o3, We1, be1, We2, be2, out):
@@ -55,23 +58,21 @@ def tile_tensor_fusion_pa_kernel(tc, o1, o2, o3, We1, be1, We2, be2, out):
                 tiles.append((j, m))
                 for r in range(starts[j], starts[j] + n):
                     jobs.append((j, m, r))
-        LAST = ROUNDS - 1
-        complete_slot = {}
+        complete = {}
         for k, job in enumerate(jobs):
-            complete_slot[job[2]] = k // 4
+            complete[job[2]] = k
 
-        oraw = const.tile([P, 3, DP], BF16, name="oraw")
-        nc.sync.dma_start(out=oraw[:, 1, 0:31], in_=o2)
-        nc.sync.dma_start(out=oraw[:, 2, 0:31], in_=o3)
-        nc.sync.dma_start(out=oraw[:, 0, 0:31], in_=o1)
-        ident_b = const.tile([P, P], BF16, name="ident_b")
-        make_identity(nc, ident_b[:])
-        ident_f = const.tile([P, P], F32, name="ident_f")
-        make_identity(nc, ident_f[:])
-        dz = const.tile([P, F], BF16, name="dz")
-        nc.vector.memset(dz[:], 0.0)
         p_all = const.tile([P, 3, DP], BF16, name="p_all")
         nc.vector.memset(p_all[:], 1.0)
+        nc.scalar.dma_start(out=p_all[:, 1, 0:31], in_=o2)
+        nc.scalar.dma_start(out=p_all[:, 2, 0:31], in_=o3)
+        nc.scalar.dma_start(out=p_all[:, 0, 0:31], in_=o1)
+        dz = const.tile([P, F], BF16, name="dz")
+        nc.vector.memset(dz[:], 0.0)
+        ident_f = const.tile([P, P], F32, name="ident_f")
+        make_identity(nc, ident_f[:])
+        ident_b = const.tile([P, P], BF16, name="ident_b")
+        make_identity(nc, ident_b[:])
         for k in range(WARM):
             xd = tps.tile([P, F], F32, name="xd", tag="xt")
             nc.tensor.matmul(out=xd[:], lhsT=dz[:, 0:P], rhs=dz[:], start=True, stop=True)
@@ -80,7 +81,7 @@ def tile_tensor_fusion_pa_kernel(tc, o1, o2, o3, We1, be1, We2, be2, out):
         be2B = const.tile([P, M], BF16, name="be2B")
 
         wviews = {}
-        st = {"tile": 0, "done": -1, "job": 0, "f": 0, "q": 0, "pend_pb": [], "pend_pg": []}
+        st = {"tile": 0, "done": -1, "job": 0, "f": 0, "q": 0, "pend_pb": [], "pend_pg": [], "s": 0}
 
         def emit_loads():
             while st["tile"] < len(tiles) and st["tile"] <= st["done"] + W_BUFS:
@@ -99,15 +100,14 @@ def tile_tensor_fusion_pa_kernel(tc, o1, o2, o3, We1, be1, We2, be2, out):
                         in_=We1[P * m:P * m + P, starts[j] * 1024:(starts[j] + n) * 1024],
                     )
                 wviews[(j, m)] = wt[:].bitcast(F32)
-                if st["tile"] == 23:
+                st["tile"] += 1
+                if st["tile"] == len(tiles):
                     nc.sync.dma_start(out=w2raw[:], in_=We2.rearrange("(a p) f -> p a f", p=P))
                     nc.sync.dma_start(out=be1B[:], in_=be1.partition_broadcast(P))
                     nc.sync.dma_start(out=be2B[:], in_=be2.partition_broadcast(P))
-                st["tile"] += 1
 
         emit_loads()
 
-        nc.vector.tensor_copy(out=p_all[:, :, 0:31], in_=oraw[:, :, 0:31])
         gb = const.tile([P, 1024], F32, name="gb")
         for w in range(4):
             nc.vector.tensor_tensor(
@@ -150,17 +150,21 @@ def tile_tensor_fusion_pa_kernel(tc, o1, o2, o3, We1, be1, We2, be2, out):
 
         gT = const.tile([P, 2048], F32, name="gT")
         gT4 = gT[:].rearrange("p (w n e) -> p w n e", w=4, e=2)
+        xgs = {}
 
         def emit_gt(jh):
             xg = tps.tile([P, 4, B], F32, name="xg", tag="xt")
             for t in range(4):
                 c0 = 512 * jh + 128 * t
                 nc.tensor.transpose(out=xg[:, t, :], in_=gb[:, c0:c0 + 128], identity=ident_f[:])
+            xgs[jh] = xg
+
+        def emit_gc(jh):
             for wl in range(2):
                 w = 2 * jh + wl
                 nc.vector.tensor_copy(
                     out=gT[:, 512 * w:512 * w + 512].rearrange("p (b u e) -> p b u e", u=2, e=2),
-                    in_=xg[:, 2 * wl:2 * wl + 2, :].rearrange("p e b -> p b e").unsqueeze(2).broadcast_to([P, B, 2, 2]),
+                    in_=xgs[jh][:, 2 * wl:2 * wl + 2, :].rearrange("p e b -> p b e").unsqueeze(2).broadcast_to([P, B, 2, 2]),
                 )
 
         w2g = const.tile([P, 4 * M], BF16, name="w2g", align_bytes=64)
@@ -200,9 +204,9 @@ def tile_tensor_fusion_pa_kernel(tc, o1, o2, o3, We1, be1, We2, be2, out):
                 op=ALU.mult,
             )
             if (i + 5) % 4 == 0 and 2 <= (i + 5) // 4 < 8:
-                st["pend_pb"] = st["pend_pb"] + [(i + 5) // 4]
+                st["pend_pb"].append((st["s"], (i + 5) // 4))
             if i % 8 == 3 and i < 24:
-                st["pend_pg"] = st["pend_pg"] + [(i + 5) // 8]
+                st["pend_pg"].append((st["s"], (i + 5) // 8))
 
         def emit_qf(i):
             fc = fpool.tile([P, 256], U32, name="fc", tag="fc", align_bytes=64)
@@ -279,64 +283,71 @@ def tile_tensor_fusion_pa_kernel(tc, o1, o2, o3, We1, be1, We2, be2, out):
                     stop=(g == 2 * ROUNDS - 1),
                 )
 
-        emit_pb(0)
+        emit_job()
         emit_gt(0)
+        emit_gc(0)
+        emit_pb(0)
         emit_job()
         emit_gt(1)
         emit_pg(0)
-        for k in range(3):
-            emit_job()
+        emit_fg(0)
+        emit_gc(1)
+        emit_fg(1)
+        emit_job()
+        emit_job()
         emit_pb(1)
-        for i in range(STAGE):
-            emit_fg(i)
 
-        for s in range(ROUNDS):
-            if s == 12:
-                emit_w2t()
+        pend_m = []
+        s = 0
+        while st["q"] < ROUNDS:
+            while pend_m and pend_m[0][0] <= s - MLAG:
+                emit_m(pend_m.pop(0)[1])
+            while st["pend_pb"] and st["pend_pb"][0][0] <= s - PLAG:
+                emit_pb(st["pend_pb"].pop(0)[1])
+            while st["pend_pg"] and st["pend_pg"][0][0] <= s - PLAG:
+                emit_pg(st["pend_pg"].pop(0)[1])
+            ready = st["job"]
             for k in range(4):
                 emit_job()
+            if ready < len(jobs) <= st["job"]:
+                emit_w2t()
             units = []
             nq = st["q"]
             nf = st["f"]
             for u in range(2):
                 f_left = nf < ROUNDS
-                can_q = nq < ROUNDS and (complete_slot[nq] < s or (not f_left and complete_slot[nq] <= s))
-                if (u == 0 and can_q) or not f_left:
+                can_q = nq < ROUNDS and (complete[nq] < ready or (not f_left and complete[nq] < st["job"]))
+                if can_q and (u == 0 or not f_left):
                     units.append(("q", nq))
                     nq += 1
-                else:
+                elif f_left:
                     units.append(("f", nf))
                     nf += 1
             st["q"] = nq
             st["f"] = nf
-            done_q = []
             for kind, x in units:
                 if kind == "f":
                     emit_qf(x)
             for kind, x in units:
                 if kind == "q":
                     emit_qw(x)
-                    done_q.append(x)
+                    pend_m.append((s, x))
             for kind, x in units:
                 if kind == "f":
                     emit_fg(x + STAGE)
-            if s == 13:
-                nc.vector.quantize_mx(out=w2c[:].bitcast(FP8X4), scales=w2s[:], in_=w2g[:])
-            for q in done_q:
-                emit_m(q)
-            for c in st["pend_pb"]:
-                emit_pb(c)
-            st["pend_pb"] = []
-            for c in st["pend_pg"]:
-                emit_pg(c)
-            st["pend_pg"] = []
-        assert st["q"] == ROUNDS and st["f"] == ROUNDS
+            s += 1
+            st["s"] = s
+        for x in pend_m:
+            emit_m(x[1])
 
         hs = const.tile([P, F], BF16, name="hs")
-        nc.vector.tensor_tensor(out=hs[:], in0=hacc[:], in1=be1B[:], op=ALU.add)
         xh = tps.tile([P, 4, B], BF16, name="xh", tag="xt")
         for t in range(4):
+            c = slice(128 * t, 128 * t + 128)
+            nc.vector.tensor_tensor(out=hs[:, c], in0=hacc[:, c], in1=be1B[:, c], op=ALU.add)
+        for t in range(4):
             nc.tensor.transpose(out=xh[:, t, :], in_=hs[:, 128 * t:128 * t + 128], identity=ident_b[:])
+        nc.vector.quantize_mx(out=w2c[:].bitcast(FP8X4), scales=w2s[:], in_=w2g[:])
         hg = const.tile([P, 4 * B], BF16, name="hg", align_bytes=64)
         nc.vector.tensor_scalar_max(
             out=hg[:].rearrange("p (b t) -> p b t", t=4),
@@ -357,6 +368,9 @@ def tile_tensor_fusion_pa_kernel(tc, o1, o2, o3, We1, be1, We2, be2, out):
             stop=True,
         )
         ot = const.tile([P, M], F32, name="ot")
-        nc.vector.tensor_tensor(out=ot[:], in0=o2ps[:], in1=be2B[:], op=ALU.add)
-        nc.vector.tensor_scalar_max(out=ot[:], in0=ot[:], scalar1=0.0)
+        halves = (slice(0, M // 2), slice(M // 2, M))
+        for c in halves:
+            nc.vector.tensor_tensor(out=ot[:, c], in0=o2ps[:, c], in1=be2B[:, c], op=ALU.add)
+        for c in halves:
+            nc.vector.tensor_scalar_max(out=ot[:, c], in0=ot[:, c], scalar1=0.0)
         nc.sync.dma_start(out=out, in_=ot[:])

from contextlib import ExitStack

import concourse.mybir as mybir
from concourse.masks import make_identity

F32 = mybir.dt.float32
BF16 = mybir.dt.bfloat16
U32 = mybir.dt.uint32
U8 = mybir.dt.uint8
FP8X4 = mybir.dt.float8_e4m3fn_x4
ALU = mybir.AluOpType

P = 128
B = 128
DP = 32
F = 512
M = 256
FUSED = DP * DP * DP
FLOPS = 2 * B * FUSED * F + 2 * B * F * M

ROUNDS = 32
LAST = ROUNDS - 1
RANGES = [1, 1, 2, 4, 4, 4, 4, 4, 4, 2, 1, 1]
W_BUFS = 8
G_BUFS = 9
STAGE = 2
BG = 40
BV = B - BG
WARM = 4
PLAG = 2
MLAG = 2


def tile_tensor_fusion_pa_kernel(tc, o1, o2, o3, We1, be1, We2, be2, out):
    nc = tc.nc
    with ExitStack() as ctx:
        ctx.enter_context(tc.manual_schedule())
        const = ctx.enter_context(tc.tile_pool(name="const", bufs=1))
        wpool = ctx.enter_context(tc.tile_pool(name="wpool", bufs=W_BUFS))
        gpool = ctx.enter_context(tc.tile_pool(name="grouped", bufs=G_BUFS))
        cpool = ctx.enter_context(tc.tile_pool(name="wcodes", bufs=6))
        spool = ctx.enter_context(tc.tile_pool(name="fstage", bufs=STAGE))
        fpool = ctx.enter_context(tc.tile_pool(name="fcodes", bufs=14))
        hps = ctx.enter_context(tc.psum_pool(name="hps", bufs=1))
        pbps = ctx.enter_context(tc.psum_pool(name="pbps", bufs=2))
        tps = ctx.enter_context(tc.psum_pool(name="tps", bufs=5))

        starts = []
        total = 0
        for n in RANGES:
            starts.append(total)
            total += n
        assert total == ROUNDS
        tiles = []
        jobs = []
        for j, n in enumerate(RANGES):
            for m in range(4):
                tiles.append((j, m))
                for r in range(starts[j], starts[j] + n):
                    jobs.append((j, m, r))
        complete = {}
        for k, job in enumerate(jobs):
            complete[job[2]] = k

        p_all = const.tile([P, 3, DP], BF16, name="p_all")
        nc.vector.memset(p_all[:], 1.0)
        nc.scalar.dma_start(out=p_all[:, 1, 0:31], in_=o2)
        nc.scalar.dma_start(out=p_all[:, 2, 0:31], in_=o3)
        nc.scalar.dma_start(out=p_all[:, 0, 0:31], in_=o1)
        dz = const.tile([P, F], BF16, name="dz")
        nc.vector.memset(dz[:], 0.0)
        ident_f = const.tile([P, P], F32, name="ident_f")
        make_identity(nc, ident_f[:])
        ident_b = const.tile([P, P], BF16, name="ident_b")
        make_identity(nc, ident_b[:])
        for k in range(WARM):
            xd = tps.tile([P, F], F32, name="xd", tag="xt")
            nc.tensor.matmul(out=xd[:], lhsT=dz[:, 0:P], rhs=dz[:], start=True, stop=True)
        w2raw = const.tile([P, 2, F], BF16, name="w2raw")
        be1B = const.tile([P, F], BF16, name="be1B")
        be2B = const.tile([P, M], BF16, name="be2B")

        wviews = {}
        st = {"tile": 0, "done": -1, "job": 0, "f": 0, "q": 0, "pend_pb": [], "pend_pg": [], "s": 0}

        def emit_loads():
            while st["tile"] < len(tiles) and st["tile"] <= st["done"] + W_BUFS:
                j, m = tiles[st["tile"]]
                n = RANGES[j]
                wt = wpool.tile([P, n * 1024], BF16, name="wt", tag="wt")
                if n == 1:
                    q, h = starts[j] // 2, starts[j] % 2
                    nc.sync.dma_start(
                        out=wt[:].rearrange("p (u c) -> p u c", u=2),
                        in_=We1[P * m:P * m + P, 2048 * q:2048 * q + 2048].rearrange("r (u c) -> r u c", u=2)[:, :, 512 * h:512 * h + 512],
                    )
                else:
                    nc.sync.dma_start(
                        out=wt[:],
                        in_=We1[P * m:P * m + P, starts[j] * 1024:(starts[j] + n) * 1024],
                    )
                wviews[(j, m)] = wt[:].bitcast(F32)
                st["tile"] += 1
                if st["tile"] == len(tiles):
                    nc.sync.dma_start(out=w2raw[:], in_=We2.rearrange("(a p) f -> p a f", p=P))
                    nc.sync.dma_start(out=be1B[:], in_=be1.partition_broadcast(P))
                    nc.sync.dma_start(out=be2B[:], in_=be2.partition_broadcast(P))

        emit_loads()

        gb = const.tile([P, 1024], F32, name="gb")
        for w in range(4):
            nc.vector.tensor_tensor(
                out=gb[:, 256 * w:256 * w + 256].rearrange("p (e j k) -> p e j k", e=2, j=8),
                in0=p_all[:, 1, 8 * w:8 * w + 8].unsqueeze(1).unsqueeze(3).broadcast_to([P, 2, 8, 16]),
                in1=p_all[:, 2, :].rearrange("p (k e) -> p e k", e=2).unsqueeze(2).broadcast_to([P, 2, 8, 16]),
                op=ALU.mult,
            )

        pbs = {}
        pgs = {}

        def emit_pb(c):
            pb = pbps.tile([P, 2, 2 * B], F32, name="pb", tag="pb")
            pbs[c] = pb
            for il in range(4):
                i = 4 * c + il
                nc.tensor.matmul(
                    out=pb[:, il // 2, il % 2:2 * B:2],
                    lhsT=p_all[:, 0, i:i + 1].to_broadcast([P, P]),
                    rhs=ident_b[:],
                    start=True,
                    stop=True,
                )

        def emit_pg(c):
            xpg = tps.tile([P, 4, 2 * BG], F32, name="xpg", tag="xt")
            for il in range(8):
                i = 8 * c + il
                nc.tensor.matmul(
                    out=xpg[:, il // 2, il % 2:2 * BG:2],
                    lhsT=p_all[:, 0, i:i + 1].to_broadcast([P, P]),
                    rhs=ident_b[:, BV:B],
                    start=True,
                    stop=True,
                )
            pg = const.tile([P, 4, 2 * BG], BF16, name="pg%d" % c)
            nc.scalar.copy(out=pg[:], in_=xpg[:])
            pgs[c] = pg

        gT = const.tile([P, 2048], F32, name="gT")
        gT4 = gT[:].rearrange("p (w n e) -> p w n e", w=4, e=2)
        xgs = {}

        def emit_gt(jh):
            xg = tps.tile([P, 4, B], F32, name="xg", tag="xt")
            for t in range(4):
                c0 = 512 * jh + 128 * t
                nc.tensor.transpose(out=xg[:, t, :], in_=gb[:, c0:c0 + 128], identity=ident_f[:])
            xgs[jh] = xg

        def emit_gc(jh):
            for wl in range(2):
                w = 2 * jh + wl
                nc.vector.tensor_copy(
                    out=gT[:, 512 * w:512 * w + 512].rearrange("p (b u e) -> p b u e", u=2, e=2),
                    in_=xgs[jh][:, 2 * wl:2 * wl + 2, :].rearrange("p e b -> p b e").unsqueeze(2).broadcast_to([P, B, 2, 2]),
                )

        w2g = const.tile([P, 4 * M], BF16, name="w2g", align_bytes=64)
        w2c = const.tile([P, M], U32, name="w2c", align_bytes=64)
        w2s = const.tile([P, M], U8, name="w2s", align_bytes=64)

        def emit_w2t():
            x2 = tps.tile([P, 2, 4, P], BF16, name="x2", tag="xt")
            for a in range(2):
                for t in range(4):
                    nc.tensor.transpose(out=x2[:, a, t, :], in_=w2raw[:, a, 128 * t:128 * t + 128], identity=ident_b[:])
            nc.scalar.copy(
                out=w2g[:].rearrange("p (a f t) -> p a f t", a=2, t=4),
                in_=x2[:].rearrange("p a t f -> p a f t"),
            )

        fstages = {}
        fcodes = {}

        def emit_fg(i):
            if i >= ROUNDS:
                return
            fst = spool.tile([P, 1024], BF16, name="fst", tag="fst", align_bytes=64)
            fstages[i] = fst
            f4 = fst[:].rearrange("p (j n e) -> p j n e", j=2, e=2)
            q, h = i // 2, i % 2
            nc.vector.tensor_tensor(
                out=f4[:, :, 0:2 * BV, :],
                in0=gT4[:, 2 * h:2 * h + 2, 0:2 * BV, :],
                in1=pbs[q // 2][:, q % 2, 0:2 * BV].unsqueeze(1).unsqueeze(3).broadcast_to([P, 2, 2 * BV, 2]),
                op=ALU.mult,
            )
            nc.gpsimd.tensor_tensor(
                out=f4[:, :, 2 * BV:2 * B, :],
                in0=gT4[:, 2 * h:2 * h + 2, 2 * BV:2 * B, :],
                in1=pgs[q // 4][:, q % 4, :].unsqueeze(1).unsqueeze(3).broadcast_to([P, 2, 2 * BG, 2]),
                op=ALU.mult,
            )
            if (i + 5) % 4 == 0 and 2 <= (i + 5) // 4 < 8:
                st["pend_pb"].append((st["s"], (i + 5) // 4))
            if i % 8 == 3 and i < 24:
                st["pend_pg"].append((st["s"], (i + 5) // 8))

        def emit_qf(i):
            fc = fpool.tile([P, 256], U32, name="fc", tag="fc", align_bytes=64)
            fs = fpool.tile([P, 256], U8, name="fs", tag="fs", align_bytes=64)
            nc.vector.quantize_mx(out=fc[:].bitcast(FP8X4), scales=fs[:], in_=fstages[i][:])
            fcodes[i] = (fc, fs)

        groupeds = {}
        wcodes = {}

        def emit_job():
            if st["job"] >= len(jobs):
                return
            j, m, r = jobs[st["job"]]
            st["job"] += 1
            if RANGES[j] == 1:
                c00, ustep = 0, 256
            else:
                c00, ustep = (r // 2 * 2 - starts[j]) * 512 + 256 * (r % 2), 512
            if m == 0:
                groupeds[r] = gpool.tile([P, 4096], BF16, name="grouped", tag="grouped", align_bytes=64)
            gw = groupeds[r][:].bitcast(F32).rearrange("p (j f u) -> p j f u", j=2, u=2)
            xt = tps.tile([P, 2, 2, P], F32, name="xt", tag="xt")
            if r == LAST:
                jh, h = m // 2, m % 2
                for u in range(2):
                    for a in range(2):
                        c0 = c00 + ustep * u + 128 * jh
                        nc.tensor.transpose(out=xt[:, u, a, :], in_=wviews[(j, 2 * h + a)][:, c0:c0 + 128], identity=ident_f[:])
                nc.scalar.copy(
                    out=gw[:, jh, 256 * h:256 * h + 256, :],
                    in_=xt[:].rearrange("p u a f -> p (a f) u"),
                )
                return
            ww = wviews[(j, m)]
            for jh in range(2):
                for u in range(2):
                    c0 = c00 + ustep * u + 128 * jh
                    nc.tensor.transpose(out=xt[:, jh, u, :], in_=ww[:, c0:c0 + 128], identity=ident_f[:])
            nc.scalar.copy(
                out=gw[:, :, P * m:P * m + P, :],
                in_=xt[:].rearrange("p j u f -> p j f u"),
            )
            if st["job"] == len(jobs) or jobs[st["job"]][0:2] != (j, m):
                st["done"] += 1
                emit_loads()

        def emit_qw(r):
            widths = [1024] if r != LAST else [512, 512]
            g = 2 * r
            for wd in widths:
                wc = cpool.tile([P, wd], U32, name="wc", tag="wc", align_bytes=64)
                ws = cpool.tile([P, wd], U8, name="ws", tag="ws", align_bytes=64)
                lo = (g - 2 * r) * 2048
                nc.vector.quantize_mx(out=wc[:].bitcast(FP8X4), scales=ws[:], in_=groupeds[r][:, lo:lo + 4 * wd])
                for x in range(wd // 512):
                    wcodes[g] = (wc[:, 512 * x:512 * x + 512], ws[:, 512 * x:512 * x + 512])
                    g += 1

        hacc = hps.tile([P, F], F32, name="hacc")

        def emit_m(r):
            fc, fs = fcodes[r]
            for jh in range(2):
                g = 2 * r + jh
                wc, ws = wcodes[g]
                nc.tensor.matmul_mx(
                    out=hacc[:],
                    lhsT=fc[:, 128 * jh:128 * jh + 128].bitcast(FP8X4),
                    lhsT_scale=fs[:, 128 * jh:128 * jh + 128],
                    rhs=wc.bitcast(FP8X4),
                    rhs_scale=ws,
                    start=(g == 0),
                    stop=(g == 2 * ROUNDS - 1),
                )

        emit_job()
        emit_gt(0)
        emit_gc(0)
        emit_pb(0)
        emit_job()
        emit_gt(1)
        emit_pg(0)
        emit_fg(0)
        emit_gc(1)
        emit_fg(1)
        emit_job()
        emit_job()
        emit_pb(1)

        pend_m = []
        s = 0
        while st["q"] < ROUNDS:
            while pend_m and pend_m[0][0] <= s - MLAG:
                emit_m(pend_m.pop(0)[1])
            while st["pend_pb"] and st["pend_pb"][0][0] <= s - PLAG:
                emit_pb(st["pend_pb"].pop(0)[1])
            while st["pend_pg"] and st["pend_pg"][0][0] <= s - PLAG:
                emit_pg(st["pend_pg"].pop(0)[1])
            ready = st["job"]
            for k in range(4):
                emit_job()
            if ready < len(jobs) <= st["job"]:
                emit_w2t()
            units = []
            nq = st["q"]
            nf = st["f"]
            for u in range(2):
                f_left = nf < ROUNDS
                can_q = nq < ROUNDS and (complete[nq] < ready or (not f_left and complete[nq] < st["job"]))
                if can_q and (u == 0 or not f_left):
                    units.append(("q", nq))
                    nq += 1
                elif f_left:
                    units.append(("f", nf))
                    nf += 1
            st["q"] = nq
            st["f"] = nf
            for kind, x in units:
                if kind == "f":
                    emit_qf(x)
            for kind, x in units:
                if kind == "q":
                    emit_qw(x)
                    pend_m.append((s, x))
            for kind, x in units:
                if kind == "f":
                    emit_fg(x + STAGE)
            s += 1
            st["s"] = s
        for x in pend_m:
            emit_m(x[1])

        hs = const.tile([P, F], BF16, name="hs")
        xh = tps.tile([P, 4, B], BF16, name="xh", tag="xt")
        for t in range(4):
            c = slice(128 * t, 128 * t + 128)
            nc.vector.tensor_tensor(out=hs[:, c], in0=hacc[:, c], in1=be1B[:, c], op=ALU.add)
        for t in range(4):
            nc.tensor.transpose(out=xh[:, t, :], in_=hs[:, 128 * t:128 * t + 128], identity=ident_b[:])
        nc.vector.quantize_mx(out=w2c[:].bitcast(FP8X4), scales=w2s[:], in_=w2g[:])
        hg = const.tile([P, 4 * B], BF16, name="hg", align_bytes=64)
        nc.vector.tensor_scalar_max(
            out=hg[:].rearrange("p (b t) -> p b t", t=4),
            in0=xh[:].rearrange("p t b -> p b t"),
            scalar1=0.0,
        )
        hc = const.tile([P, B], U32, name="hc", align_bytes=64)
        hsc = const.tile([P, B], U8, name="hsc", align_bytes=64)
        nc.vector.quantize_mx(out=hc[:].bitcast(FP8X4), scales=hsc[:], in_=hg[:])
        o2ps = tps.tile([P, M], F32, name="o2ps", tag="xt")
        nc.tensor.matmul_mx(
            out=o2ps[:],
            lhsT=hc[:].bitcast(FP8X4),
            lhsT_scale=hsc[:],
            rhs=w2c[:].bitcast(FP8X4),
            rhs_scale=w2s[:],
            start=True,
            stop=True,
        )
        ot = const.tile([P, M], F32, name="ot")
        halves = (slice(0, M // 2), slice(M // 2, M))
        for c in halves:
            nc.vector.tensor_tensor(out=ot[:, c], in0=o2ps[:, c], in1=be2B[:, c], op=ALU.add)
        for c in halves:
            nc.vector.tensor_scalar_max(out=ot[:, c], in0=ot[:, c], scalar1=0.0)
        nc.sync.dma_start(out=out, in_=ot[:])
